import numpy as np
import ml_dtypes


def mxq(x, axis, fmt="e4m3"):
    dtype, down = {"e4m3": (ml_dtypes.float8_e4m3fn, 7), "e5m2": (ml_dtypes.float8_e5m2, 14)}[fmt]
    v = np.moveaxis(np.asarray(x, np.float32).astype(ml_dtypes.bfloat16).astype(np.float64), axis, -1)
    blocks = v.reshape(v.shape[:-1] + (-1, 32))
    amax = np.abs(blocks).max(-1, keepdims=True)
    byte = np.maximum(np.where(amax > 0, np.frexp(amax)[1] - 1 + 127, 0) - down, 1)
    scale = np.exp2(byte - 127.0)
    codes = (blocks / scale).astype(np.float32).astype(dtype).astype(np.float64)
    return np.moveaxis((codes * scale).reshape(v.shape), -1, axis)


WIDE = False


def mx_kscale(k):
    if not WIDE:
        return np.ones(k)
    levels = np.array([10, -10, 5, -5, 0])
    a = np.random.permutation(np.resize(levels, k // 512 * 4)).reshape(k // 512, 4)
    idx = np.arange(k)
    return np.exp2(a[idx // 512, idx % 128 // 32])


BF16 = ml_dtypes.bfloat16


def bf(x):
    return np.asarray(x, np.float32).astype(BF16)


def f64(x):
    return np.asarray(x).astype(np.float64)


B, T, D, N, R = 2, 512, 512, 4096, 32

MAX_ATTENTION_SCALE = 1.0
MIN_ATTENTION_SCALE = 0.05
SCALE_GROWTH_RATE = 0.02
G = 4.0
C0 = 12.0


def cloud(rows, u):
    z = np.random.standard_normal((rows, R))
    return (z @ u / np.sqrt(R) + np.random.standard_normal((rows, D))) * (G / np.sqrt(2.0 * D))


def setup_inputs():
    t = mx_kscale(N)
    u = np.random.standard_normal((R, D))
    x = cloud(B * T, u).reshape(B, T, D)
    positions = cloud(N, u)
    c = C0 * (1.0 + 0.03 * np.random.standard_normal(N)) - np.log(t)
    sign = np.where(np.random.standard_normal(N) < 0.0, -1.0, 1.0)
    temperature = sign * (np.sqrt(2.0) * G / c / MIN_ATTENTION_SCALE - 0.1)
    values = np.random.standard_normal((N, D)) * 0.15 * np.sqrt(N) * (t.mean() / t)[:, None]
    return {"x": bf(x), "positions": bf(positions), "values": bf(values), "temperature": bf(temperature)}


def reference(x, positions, values, temperature):
    x, positions, values, temperature = f64(x), f64(positions), f64(values), f64(temperature)
    Bb, Tt, Dd = x.shape
    ages = np.zeros((positions.shape[0],))
    attention_scale = MIN_ATTENTION_SCALE + (MAX_ATTENTION_SCALE - MIN_ATTENTION_SCALE) * (1.0 - np.exp(-SCALE_GROWTH_RATE * ages))
    x_flat = x.reshape(-1, Dd)
    x2 = np.sum(x_flat * x_flat, axis=-1, keepdims=True)
    p2 = np.sum(positions * positions, axis=-1)[None, :]
    sq = x2 + p2 - 2.0 * (mxq(x_flat, 1, "e4m3") @ mxq(positions, 1, "e4m3").T)
    dists = np.sqrt(np.maximum(sq, 0.0))
    effective_temp = (np.abs(temperature) + 0.1) * attention_scale
    weights = np.exp(-dists / effective_temp[None, :])
    weights = weights / (np.sum(weights, axis=-1, keepdims=True) + 1e-8)
    out = mxq(weights, 1, "e4m3") @ mxq(values, 0, "e4m3")
    return out.reshape(Bb, Tt, Dd)

@@ -1,0 +1,344 @@
+from contextlib import ExitStack
+
+import concourse.mybir as mybir
+from concourse.masks import make_identity
+
+F32 = mybir.dt.float32
+BF16 = mybir.dt.bfloat16
+U32 = mybir.dt.uint32
+U8 = mybir.dt.uint8
+FP8X4 = mybir.dt.float8_e4m3fn_x4
+ALU = mybir.AluOpType
+ACT = mybir.ActivationFunctionType
+
+P = 128
+D = 512
+ROWS = 1024
+ANCH = 4096
+CHUNK = 512
+N_RT = ROWS // P
+N_CH = ANCH // CHUNK
+N_GR = ROWS // CHUNK
+
+CLAMP_ON_G = True
+VAL_LATE = 3
+
+FLOPS = 2 * 2 * ROWS * ANCH * D
+
+
+def tile_multiscalegeometricattention_kernel(tc, x, positions, values, temperature, out):
+    nc = tc.nc
+    xf = x.flatten_outer_dims()
+    of = out.flatten_outer_dims().rearrange("(g m i) d -> g i m d", g=N_GR, i=4)
+
+    with ExitStack() as ctx:
+        const = ctx.enter_context(tc.tile_pool(name="const", bufs=1))
+        rawp = ctx.enter_context(tc.tile_pool(name="rawp", bufs=4))
+        rawv = ctx.enter_context(tc.tile_pool(name="rawv", bufs=2))
+        grp = ctx.enter_context(tc.tile_pool(name="grp", bufs=4))
+        wcp = ctx.enter_context(tc.tile_pool(name="wcp", bufs=3))
+        outp = ctx.enter_context(tc.tile_pool(name="outp", bufs=2))
+        psum = ctx.enter_context(tc.psum_pool(name="psum", bufs=8))
+        ctx.enter_context(tc.manual_schedule())
+
+        temp_b = const.tile([P, 4 * N_CH], BF16)
+        nc.scalar.dma_start(
+            out=temp_b[:].rearrange("p (c t) -> p c t", t=4), in_=temperature.rearrange("(c p t) -> p c t", p=P, t=4)
+        )
+        warm = const.tile([P, 1], F32)
+        nc.vector.memset(warm[:], 1.0)
+        nc.scalar.activation(out=warm[:], in_=warm[:], func=ACT.Sqrt)
+        ident_f = const.tile([P, P], F32)
+        make_identity(nc, ident_f[:])
+
+        xc = const.tile([P, ROWS], U32, align_bytes=64)
+        xs = const.tile([P, ROWS], U8, align_bytes=64)
+        pc = const.tile([P, ANCH], U32, align_bytes=64)
+        ps = const.tile([P, ANCH], U8, align_bytes=64)
+        vc = const.tile([P, N_CH * D], U32, align_bytes=64)
+        vs = const.tile([P, N_CH * D], U8, align_bytes=64)
+        x2 = const.tile([P, N_RT], F32)
+        nhx2 = const.tile([P, N_RT], F32)
+        p2 = const.tile([P, 4 * N_CH], F32)
+        nhp2 = const.tile([P, 4 * N_CH], F32)
+        nhx2b = const.tile([P, ROWS], F32)
+        rsum = const.tile([P, N_RT], F32)
+        rinv = const.tile([P, N_RT], F32)
+        junk_s = const.tile([P, D], BF16)
+        junk_r = const.tile([P, P], F32)
+        tau = const.tile([P, 4 * N_CH], F32)
+        m2a = const.tile([P, 4 * N_CH], F32)
+        dist = []
+        for c in range(N_CH):
+            dist.append(const.tile([P, N_RT, CHUNK], F32, name="dist%d" % c))
+
+
+        def load(pool, src):
+            raw = pool.tile([P, 4, D], BF16, tag="raw", name="raw")
+            nc.sync.dma_start(out=raw[:], in_=src.rearrange("(p i) d -> p i d", i=4))
+            return raw
+
+        def squares(raw, sums):
+            for i in range(4):
+                nc.scalar.activation(out=junk_s[:], in_=raw[:, i, :], func=ACT.Square, accum_out=sums[:, i : i + 1])
+
+        def word_transposes(raw):
+            words = raw[:].bitcast(F32)
+            banks = []
+            for b in range(2):
+                bank = psum.tile([P, 512], F32, tag="bank", name="wbank")
+                for ii in range(2):
+                    for u in range(2):
+                        s = 2 * ii + u
+                        nc.tensor.transpose(bank[:, s * P : (s + 1) * P], words[:, 2 * b + ii, u * P : (u + 1) * P], ident_f[:])
+                banks.append(bank)
+            return banks
+
+        def copy_out(on_vector, banks):
+            grouped = grp.tile([P, 4 * CHUNK], BF16, tag="grouped", name="grouped", align_bytes=64)
+            gwords = grouped[:].bitcast(F32)
+            for b in range(2):
+                dst = gwords[:, 512 * b : 512 * (b + 1)].rearrange("q (i m u) -> q i m u", i=2, u=2)
+                src = banks[b][:].rearrange("q (i u m) -> q i m u", i=2, u=2)
+                if on_vector:
+                    nc.vector.tensor_copy(out=dst, in_=src)
+                else:
+                    nc.scalar.copy(out=dst, in_=src)
+            return grouped
+
+        def quantise(grouped, codes, scales):
+            nc.vector.quantize_mx(out=codes.bitcast(FP8X4), scales=scales, in_=grouped[:])
+
+        def spread_x2(g):
+            bbank = psum.tile([P, 512], F32, tag="bank", name="bbank")
+            for i in range(4):
+                t = 4 * g + i
+                nc.tensor.matmul(
+                    out=bbank[:, i * P : (i + 1) * P],
+                    lhsT=nhx2[:, t : t + 1].to_broadcast([P, P]),
+                    rhs=ident_f[:],
+                    start=True,
+                    stop=True,
+                )
+            return bbank
+
+        def regroup_values(raw):
+            grouped = grp.tile([P, 4 * D], BF16, tag="grouped", name="grouped", align_bytes=64)
+            nc.vector.tensor_copy(
+                out=grouped[:].rearrange("p (c i t) -> p c t i", i=4, t=4),
+                in_=raw[:].rearrange("p t (c i) -> p c t i", i=4),
+            )
+            return grouped
+
+        pos_chunk = lambda c: positions[c * CHUNK : (c + 1) * CHUNK, :]
+        val_chunk = lambda c: values[c * CHUNK : (c + 1) * CHUNK, :]
+        raw_x0 = load(rawp, xf[0:CHUNK, :])
+        raw_p = {0: load(rawp, pos_chunk(0))}
+        raw_x1 = load(rawp, xf[CHUNK : 2 * CHUNK, :])
+        raw_p[1] = load(rawp, pos_chunk(1))
+        raw_v = {}
+
+        nc.vector.scalar_tensor_tensor(out=tau[:], in0=temp_b[:], scalar=-1.0, in1=temp_b[:], op0=ALU.mult, op1=ALU.max)
+        nc.vector.tensor_scalar(out=tau[:], in0=tau[:], scalar1=0.1, scalar2=0.05, op0=ALU.add, op1=ALU.mult)
+        nc.vector.tensor_tensor(out=m2a[:], in0=tau[:], in1=tau[:], op=ALU.mult)
+        nc.vector.reciprocal(out=m2a[:], in_=m2a[:])
+        nc.vector.tensor_scalar_mul(out=m2a[:], in0=m2a[:], scalar1=-2.0)
+        squares(raw_x0, x2[:, 0:4])
+        g_x0 = copy_out(True, word_transposes(raw_x0))
+        raw_p[2] = load(rawp, pos_chunk(2))
+        squares(raw_x1, x2[:, 4:8])
+        g_p0 = copy_out(True, word_transposes(raw_p[0]))
+        quantise(g_x0, xc[:, 0:CHUNK], xs[:, 0:CHUNK])
+        g_x1 = copy_out(True, word_transposes(raw_x1))
+        raw_p[3] = load(rawp, pos_chunk(3))
+        quantise(g_p0, pc[:, 0:CHUNK], ps[:, 0:CHUNK])
+        squares(raw_p[0], p2[:, 0:4])
+        raw_v[0] = load(rawv, val_chunk(0))
+        raw_v[1] = load(rawv, val_chunk(1))
+        nc.vector.tensor_scalar_mul(out=nhx2[:], in0=x2[:], scalar1=-0.5)
+        bb0 = spread_x2(0)
+        bb1 = spread_x2(1)
+        quantise(g_x1, xc[:, CHUNK : 2 * CHUNK], xs[:, CHUNK : 2 * CHUNK])
+        nc.vector.tensor_copy(out=nhx2b[:, 0:CHUNK], in_=bb0[:])
+        nc.vector.tensor_copy(out=nhx2b[:, CHUNK : 2 * CHUNK], in_=bb1[:])
+        nc.vector.tensor_scalar_mul(out=nhp2[:, 0:4], in0=p2[:, 0:4], scalar1=-0.5)
+
+        def product(j, g):
+            acols = slice(j * P, (j + 1) * P)
+            cols = slice(g * CHUNK, (g + 1) * CHUNK)
+            sbank = psum.tile([P, CHUNK], F32, tag="bank", name="sbank")
+            nc.tensor.matmul_mx(
+                out=sbank[:],
+                lhsT=pc[:, acols].bitcast(FP8X4),
+                lhsT_scale=ps[:, acols],
+                rhs=xc[:, cols].bitcast(FP8X4),
+                rhs_scale=xs[:, cols],
+                start=True,
+                stop=True,
+            )
+            nc.vector.scalar_tensor_tensor(
+                out=dist[j // 4][:, 4 * g : 4 * g + 4, (j % 4) * P : (j % 4 + 1) * P],
+                in0=sbank[:].rearrange("p (i m) -> p i m", i=4),
+                scalar=nhp2[:, j : j + 1],
+                in1=nhx2b[:, cols].rearrange("p (i m) -> p i m", i=4),
+                op0=ALU.add,
+                op1=ALU.add,
+            )
+
+        def clamp(j):
+            view = dist[j // 4][:, :, (j % 4) * P : (j % 4 + 1) * P]
+            if CLAMP_ON_G:
+                if j % 2 == 1:
+                    pair = dist[j // 4][:, :, (j % 4 - 1) * P : (j % 4 + 1) * P]
+                    nc.gpsimd.tensor_scalar(out=pair, in0=pair, scalar1=0.0, scalar2=-3.0e38, op0=ALU.min, op1=ALU.max)
+            else:
+                nc.vector.tensor_scalar(out=view, in0=view, scalar1=0.0, scalar2=m2a[:, j : j + 1], op0=ALU.min, op1=ALU.mult)
+
+        def root(j):
+            view = dist[j // 4][:, :, (j % 4) * P : (j % 4 + 1) * P]
+            if CLAMP_ON_G:
+                nc.scalar.activation(out=view, in_=view, func=ACT.Sqrt, scale=m2a[:, j : j + 1])
+            else:
+                nc.scalar.activation(out=view, in_=view, func=ACT.Sqrt)
+
+        g_v = {}
+
+        def values_a(c):
+            g_v[c] = regroup_values(raw_v[c])
+            if c + 2 < N_CH:
+                raw_v[c + 2] = load(rawv, val_chunk(c + 2))
+
+        def values_b(c):
+            quantise(g_v[c], vc[:, c * D : (c + 1) * D], vs[:, c * D : (c + 1) * D])
+
+        n_early = N_CH - VAL_LATE
+        for c in range(N_CH):
+            nxt = c + 1
+            if nxt < N_CH:
+                g_next = copy_out(False, word_transposes(raw_p[nxt]))
+                squares(raw_p[nxt], p2[:, 4 * nxt : 4 * nxt + 4])
+                if nxt + 3 < N_CH:
+                    raw_p[nxt + 3] = load(rawp, pos_chunk(nxt + 3))
+            for jj in range(4):
+                j = 4 * c + jj
+                product(j, 0)
+                product(j, 1)
+                clamp(j)
+                if j >= 3 and j % 2 == 1:
+                    root(j - 3)
+                    root(j - 2)
+                if jj == 1 and c < n_early:
+                    values_a(c)
+                if jj == 2 and nxt < N_CH:
+                    quantise(g_next, pc[:, nxt * CHUNK : (nxt + 1) * CHUNK], ps[:, nxt * CHUNK : (nxt + 1) * CHUNK])
+                    nc.vector.tensor_scalar_mul(
+                        out=nhp2[:, 4 * nxt : 4 * nxt + 4], in0=p2[:, 4 * nxt : 4 * nxt + 4], scalar1=-0.5
+                    )
+                if jj == 3 and c < n_early:
+                    values_b(c)
+        root(4 * N_CH - 2)
+        root(4 * N_CH - 1)
+        for c in range(n_early, N_CH):
+            values_a(c)
+            if c > n_early:
+                values_b(c - 1)
+        values_b(N_CH - 1)
+
+        acc = {}
+        rb = {}
+        gw = {}
+        wc = {}
+        ws = {}
+        obank = {}
+
+        def exps(i, chunks):
+            if i not in acc:
+                acc[i] = psum.tile([P, 512], F32, tag="bank", name="acc")
+            for c in chunks:
+                nc.scalar.activation(out=dist[c][:, i, :], in_=dist[c][:, i, :], func=ACT.Exp, scale=-1.0)
+                for t in range(4):
+                    nc.tensor.matmul(
+                        out=acc[i][:, 0:P],
+                        lhsT=dist[c][:, i, t * P : (t + 1) * P],
+                        rhs=ident_f[:],
+                        is_transpose=True,
+                        start=(c == 0 and t == 0),
+                        stop=(c == N_CH - 1 and t == 3),
+                    )
+
+        def row_sum(i):
+            nc.scalar.activation(out=junk_r[:], in_=acc[i][:, 0:P], func=ACT.Identity, accum_out=rsum[:, i : i + 1])
+
+        def inverse(i):
+            nc.vector.tensor_scalar_add(out=rinv[:, i : i + 1], in0=rsum[:, i : i + 1], scalar1=1e-8)
+            nc.vector.reciprocal(out=rinv[:, i : i + 1], in_=rinv[:, i : i + 1])
+            rb[i] = psum.tile([P, 512], F32, tag="bank", name="rb")
+            nc.tensor.matmul(
+                out=rb[i][:, 0:P], lhsT=rinv[:, i : i + 1].to_broadcast([P, P]), rhs=ident_f[:], start=True, stop=True
+            )
+
+        def weights(i, c):
+            h = c // 4
+            if c % 4 == 0:
+                gw[(i, h)] = grp.tile([P, 4 * CHUNK], BF16, tag="grouped", name="gw", align_bytes=64)
+            cc = c % 4
+            nc.vector.tensor_tensor(
+                out=gw[(i, h)][:, cc * 512 : (cc + 1) * 512].rearrange("p (m t) -> p m t", t=4),
+                in0=dist[c][:, i, :].rearrange("p (t m) -> p m t", t=4),
+                in1=rb[i][:, 0:P].unsqueeze(2).to_broadcast([P, P, 4]),
+                op=ALU.mult,
+            )
+
+        def second(i, h):
+            wc[(i, h)] = wcp.tile([P, CHUNK], U32, tag="wc", name="wc", align_bytes=64)
+            ws[(i, h)] = wcp.tile([P, CHUNK], U8, tag="ws", name="ws", align_bytes=64)
+            quantise(gw[(i, h)], wc[(i, h)][:], ws[(i, h)][:])
+            if h == 0:
+                obank[i] = psum.tile([P, D], F32, tag="bank", name="obank")
+            for cc in range(4):
+                g = 4 * h + cc
+                nc.tensor.matmul_mx(
+                    out=obank[i][:],
+                    lhsT=wc[(i, h)][:, cc * P : (cc + 1) * P].bitcast(FP8X4),
+                    lhsT_scale=ws[(i, h)][:, cc * P : (cc + 1) * P],
+                    rhs=vc[:, g * D : (g + 1) * D].bitcast(FP8X4),
+                    rhs_scale=vs[:, g * D : (g + 1) * D],
+                    start=(g == 0),
+                    stop=(g == N_CH - 1),
+                )
+
+        def store(i):
+            ost = outp.tile([P, D], F32, tag="ost", name="ost")
+            nc.scalar.copy(out=ost[:], in_=obank[i][:])
+            nc.sync.dma_start(out=of[i // 4, i % 4], in_=ost[:])
+
+        def vector_block(i):
+            weights(i, 0)
+            if i > 0:
+                second(i - 1, 1)
+            for c in range(1, 5):
+                weights(i, c)
+            second(i, 0)
+            weights(i, 5)
+            if i + 1 < N_RT:
+                inverse(i + 1)
+            weights(i, 6)
+            weights(i, 7)
+
+        exps(0, range(N_CH))
+        row_sum(0)
+        inverse(0)
+        exps(1, range(N_CH))
+        for n in range(2, N_RT + 3):
+            if n < N_RT:
+                exps(n, range(0, 2))
+            if n - 1 < N_RT:
+                row_sum(n - 1)
+            if n < N_RT:
+                exps(n, range(2, N_CH))
+            if n - 2 < N_RT:
+                vector_block(n - 2)
+            if n - 2 == N_RT:
+                second(N_RT - 1, 1)
+            if n >= 3:
+                store(n - 3)

@@ -16,12 +16,14 @@ D = 512
 ROWS = 1024
 ANCH = 4096
 CHUNK = 512
+HALF = 2048
 N_RT = ROWS // P
 N_CH = ANCH // CHUNK
 N_GR = ROWS // CHUNK
 
-CLAMP_ON_G = True
-VAL_LATE = 3
+REGROUP_ON_G = False
+VAL_LATE = 6
+HEAD_COPIES_V = True
 
 FLOPS = 2 * 2 * ROWS * ANCH * D
 
@@ -69,9 +71,8 @@ def tile_multiscalegeometricattention_kernel(tc, x, positions, values, temperatu
         tau = const.tile([P, 4 * N_CH], F32)
         m2a = const.tile([P, 4 * N_CH], F32)
         dist = []
-        for c in range(N_CH):
-            dist.append(const.tile([P, N_RT, CHUNK], F32, name="dist%d" % c))
-
+        for h in range(2):
+            dist.append(const.tile([P, N_RT, HALF], F32, name="dist%d" % h))
 
         def load(pool, src):
             raw = pool.tile([P, 4, D], BF16, tag="raw", name="raw")
@@ -124,10 +125,20 @@ def tile_multiscalegeometricattention_kernel(tc, x, positions, values, temperatu
 
         def regroup_values(raw):
             grouped = grp.tile([P, 4 * D], BF16, tag="grouped", name="grouped", align_bytes=64)
-            nc.vector.tensor_copy(
-                out=grouped[:].rearrange("p (c i t) -> p c t i", i=4, t=4),
-                in_=raw[:].rearrange("p t (c i) -> p c t i", i=4),
-            )
+            if REGROUP_ON_G:
+                nc.gpsimd.tensor_scalar(
+                    out=grouped[:].rearrange("p (d t) -> p d t", t=4),
+                    in0=raw[:].rearrange("p t d -> p d t"),
+                    scalar1=1.0,
+                    scalar2=0.0,
+                    op0=ALU.mult,
+                    op1=ALU.add,
+                )
+            else:
+                nc.vector.tensor_copy(
+                    out=grouped[:].rearrange("p (c i t) -> p c t i", i=4, t=4),
+                    in_=raw[:].rearrange("p t (c i) -> p c t i", i=4),
+                )
             return grouped
 
         pos_chunk = lambda c: positions[c * CHUNK : (c + 1) * CHUNK, :]
@@ -144,12 +155,12 @@ def tile_multiscalegeometricattention_kernel(tc, x, positions, values, temperatu
         nc.vector.reciprocal(out=m2a[:], in_=m2a[:])
         nc.vector.tensor_scalar_mul(out=m2a[:], in0=m2a[:], scalar1=-2.0)
         squares(raw_x0, x2[:, 0:4])
-        g_x0 = copy_out(True, word_transposes(raw_x0))
+        g_x0 = copy_out(HEAD_COPIES_V, word_transposes(raw_x0))
         raw_p[2] = load(rawp, pos_chunk(2))
         squares(raw_x1, x2[:, 4:8])
-        g_p0 = copy_out(True, word_transposes(raw_p[0]))
+        g_p0 = copy_out(HEAD_COPIES_V, word_transposes(raw_p[0]))
         quantise(g_x0, xc[:, 0:CHUNK], xs[:, 0:CHUNK])
-        g_x1 = copy_out(True, word_transposes(raw_x1))
+        g_x1 = copy_out(HEAD_COPIES_V, word_transposes(raw_x1))
         raw_p[3] = load(rawp, pos_chunk(3))
         quantise(g_p0, pc[:, 0:CHUNK], ps[:, 0:CHUNK])
         squares(raw_p[0], p2[:, 0:4])
@@ -162,6 +173,9 @@ def tile_multiscalegeometricattention_kernel(tc, x, positions, values, temperatu
         nc.vector.tensor_copy(out=nhx2b[:, 0:CHUNK], in_=bb0[:])
         nc.vector.tensor_copy(out=nhx2b[:, CHUNK : 2 * CHUNK], in_=bb1[:])
         nc.vector.tensor_scalar_mul(out=nhp2[:, 0:4], in0=p2[:, 0:4], scalar1=-0.5)
+
+        def block(j):
+            return dist[j // 16][:, :, (j % 16) * P : (j % 16 + 1) * P]
 
         def product(j, g):
             acols = slice(j * P, (j + 1) * P)
@@ -177,7 +191,7 @@ def tile_multiscalegeometricattention_kernel(tc, x, positions, values, temperatu
                 stop=True,
             )
             nc.vector.scalar_tensor_tensor(
-                out=dist[j // 4][:, 4 * g : 4 * g + 4, (j % 4) * P : (j % 4 + 1) * P],
+                out=block(j)[:, 4 * g : 4 * g + 4, :],
                 in0=sbank[:].rearrange("p (i m) -> p i m", i=4),
                 scalar=nhp2[:, j : j + 1],
                 in1=nhx2b[:, cols].rearrange("p (i m) -> p i m", i=4),
@@ -185,21 +199,13 @@ def tile_multiscalegeometricattention_kernel(tc, x, positions, values, temperatu
                 op1=ALU.add,
             )
 
-        def clamp(j):
-            view = dist[j // 4][:, :, (j % 4) * P : (j % 4 + 1) * P]
-            if CLAMP_ON_G:
-                if j % 2 == 1:
-                    pair = dist[j // 4][:, :, (j % 4 - 1) * P : (j % 4 + 1) * P]
-                    nc.gpsimd.tensor_scalar(out=pair, in0=pair, scalar1=0.0, scalar2=-3.0e38, op0=ALU.min, op1=ALU.max)
-            else:
-                nc.vector.tensor_scalar(out=view, in0=view, scalar1=0.0, scalar2=m2a[:, j : j + 1], op0=ALU.min, op1=ALU.mult)
+        def clamp(c, part):
+            lo = (c % 4) * CHUNK + part * 2 * P
+            view = dist[c // 4][:, :, lo : lo + 2 * P]
+            nc.vector.tensor_scalar_min(out=view, in0=view, scalar1=0.0)
 
         def root(j):
-            view = dist[j // 4][:, :, (j % 4) * P : (j % 4 + 1) * P]
-            if CLAMP_ON_G:
-                nc.scalar.activation(out=view, in_=view, func=ACT.Sqrt, scale=m2a[:, j : j + 1])
-            else:
-                nc.scalar.activation(out=view, in_=view, func=ACT.Sqrt)
+            nc.scalar.activation(out=block(j), in_=block(j), func=ACT.Sqrt, scale=m2a[:, j : j + 1])
 
         g_v = {}
 
@@ -223,19 +229,24 @@ def tile_multiscalegeometricattention_kernel(tc, x, positions, values, temperatu
                 j = 4 * c + jj
                 product(j, 0)
                 product(j, 1)
-                clamp(j)
-                if j >= 3 and j % 2 == 1:
-                    root(j - 3)
+                if jj == 0 and c > 0:
+                    clamp(c - 1, 1)
                     root(j - 2)
+                    root(j - 1)
                 if jj == 1 and c < n_early:
                     values_a(c)
-                if jj == 2 and nxt < N_CH:
-                    quantise(g_next, pc[:, nxt * CHUNK : (nxt + 1) * CHUNK], ps[:, nxt * CHUNK : (nxt + 1) * CHUNK])
-                    nc.vector.tensor_scalar_mul(
-                        out=nhp2[:, 4 * nxt : 4 * nxt + 4], in0=p2[:, 4 * nxt : 4 * nxt + 4], scalar1=-0.5
-                    )
+                if jj == 2:
+                    clamp(c, 0)
+                    root(j - 2)
+                    root(j - 1)
+                    if nxt < N_CH:
+                        quantise(g_next, pc[:, nxt * CHUNK : (nxt + 1) * CHUNK], ps[:, nxt * CHUNK : (nxt + 1) * CHUNK])
+                        nc.vector.tensor_scalar_mul(
+                            out=nhp2[:, 4 * nxt : 4 * nxt + 4], in0=p2[:, 4 * nxt : 4 * nxt + 4], scalar1=-0.5
+                        )
                 if jj == 3 and c < n_early:
                     values_b(c)
+        clamp(N_CH - 1, 1)
         root(4 * N_CH - 2)
         root(4 * N_CH - 1)
         for c in range(n_early, N_CH):
@@ -247,24 +258,23 @@ def tile_multiscalegeometricattention_kernel(tc, x, positions, values, temperatu
         acc = {}
         rb = {}
         gw = {}
-        wc = {}
-        ws = {}
         obank = {}
 
-        def exps(i, chunks):
-            if i not in acc:
+        def exps(i, h):
+            nc.scalar.activation(out=dist[h][:, i, :], in_=dist[h][:, i, :], func=ACT.Exp, scale=-1.0)
+
+        def partial_sums(i, h):
+            if h == 0:
                 acc[i] = psum.tile([P, 512], F32, tag="bank", name="acc")
-            for c in chunks:
-                nc.scalar.activation(out=dist[c][:, i, :], in_=dist[c][:, i, :], func=ACT.Exp, scale=-1.0)
-                for t in range(4):
-                    nc.tensor.matmul(
-                        out=acc[i][:, 0:P],
-                        lhsT=dist[c][:, i, t * P : (t + 1) * P],
-                        rhs=ident_f[:],
-                        is_transpose=True,
-                        start=(c == 0 and t == 0),
-                        stop=(c == N_CH - 1 and t == 3),
-                    )
+            for t in range(16):
+                nc.tensor.matmul(
+                    out=acc[i][:, 0:P],
+                    lhsT=dist[h][:, i, t * P : (t + 1) * P],
+                    rhs=ident_f[:],
+                    is_transpose=True,
+                    start=(h == 0 and t == 0),
+                    stop=(h == 1 and t == 15),
+                )
 
         def row_sum(i):
             nc.scalar.activation(out=junk_r[:], in_=acc[i][:, 0:P], func=ACT.Identity, accum_out=rsum[:, i : i + 1])
@@ -277,30 +287,27 @@ def tile_multiscalegeometricattention_kernel(tc, x, positions, values, temperatu
                 out=rb[i][:, 0:P], lhsT=rinv[:, i : i + 1].to_broadcast([P, P]), rhs=ident_f[:], start=True, stop=True
             )
 
-        def weights(i, c):
-            h = c // 4
-            if c % 4 == 0:
-                gw[(i, h)] = grp.tile([P, 4 * CHUNK], BF16, tag="grouped", name="gw", align_bytes=64)
-            cc = c % 4
+        def weights(i, h):
+            gw[(i, h)] = grp.tile([P, 4 * CHUNK], BF16, tag="grouped", name="gw", align_bytes=64)
             nc.vector.tensor_tensor(
-                out=gw[(i, h)][:, cc * 512 : (cc + 1) * 512].rearrange("p (m t) -> p m t", t=4),
-                in0=dist[c][:, i, :].rearrange("p (t m) -> p m t", t=4),
-                in1=rb[i][:, 0:P].unsqueeze(2).to_broadcast([P, P, 4]),
+                out=gw[(i, h)][:].rearrange("p (c m t) -> p c m t", c=4, t=4),
+                in0=dist[h][:, i, :].rearrange("p (c t m) -> p c m t", c=4, t=4),
+                in1=rb[i][:, 0:P].unsqueeze(1).unsqueeze(3).to_broadcast([P, 4, P, 4]),
                 op=ALU.mult,
             )
 
         def second(i, h):
-            wc[(i, h)] = wcp.tile([P, CHUNK], U32, tag="wc", name="wc", align_bytes=64)
-            ws[(i, h)] = wcp.tile([P, CHUNK], U8, tag="ws", name="ws", align_bytes=64)
-            quantise(gw[(i, h)], wc[(i, h)][:], ws[(i, h)][:])
+            wc = wcp.tile([P, CHUNK], U32, tag="wc", name="wc", align_bytes=64)
+            ws = wcp.tile([P, CHUNK], U8, tag="ws", name="ws", align_bytes=64)
+            quantise(gw[(i, h)], wc[:], ws[:])
             if h == 0:
                 obank[i] = psum.tile([P, D], F32, tag="bank", name="obank")
             for cc in range(4):
                 g = 4 * h + cc
                 nc.tensor.matmul_mx(
                     out=obank[i][:],
-                    lhsT=wc[(i, h)][:, cc * P : (cc + 1) * P].bitcast(FP8X4),
-                    lhsT_scale=ws[(i, h)][:, cc * P : (cc + 1) * P],
+                    lhsT=wc[:, cc * P : (cc + 1) * P].bitcast(FP8X4),
+                    lhsT_scale=ws[:, cc * P : (cc + 1) * P],
                     rhs=vc[:, g * D : (g + 1) * D].bitcast(FP8X4),
                     rhs_scale=vs[:, g * D : (g + 1) * D],
                     start=(g == 0),
@@ -312,33 +319,34 @@ def tile_multiscalegeometricattention_kernel(tc, x, positions, values, temperatu
             nc.scalar.copy(out=ost[:], in_=obank[i][:])
             nc.sync.dma_start(out=of[i // 4, i % 4], in_=ost[:])
 
-        def vector_block(i):
-            weights(i, 0)
-            if i > 0:
-                second(i - 1, 1)
-            for c in range(1, 5):
-                weights(i, c)
-            second(i, 0)
-            weights(i, 5)
-            if i + 1 < N_RT:
-                inverse(i + 1)
-            weights(i, 6)
-            weights(i, 7)
+        def exp_tile(i):
+            for h in range(2):
+                exps(i, h)
+                partial_sums(i, h)
 
-        exps(0, range(N_CH))
+        exp_tile(0)
         row_sum(0)
         inverse(0)
-        exps(1, range(N_CH))
-        for n in range(2, N_RT + 3):
-            if n < N_RT:
-                exps(n, range(0, 2))
-            if n - 1 < N_RT:
-                row_sum(n - 1)
-            if n < N_RT:
-                exps(n, range(2, N_CH))
-            if n - 2 < N_RT:
-                vector_block(n - 2)
-            if n - 2 == N_RT:
-                second(N_RT - 1, 1)
-            if n >= 3:
-                store(n - 3)
+        exp_tile(1)
+        exps(2, 0)
+        row_sum(1)
+        exps(2, 1)
+        for i in range(N_RT):
+            weights(i, 0)
+            weights(i, 1)
+            if i + 1 < N_RT:
+                inverse(i + 1)
+            if i + 2 < N_RT:
+                partial_sums(i + 2, 0)
+                partial_sums(i + 2, 1)
+            if i + 3 < N_RT:
+                exps(i + 3, 0)
+            if i + 2 < N_RT:
+                row_sum(i + 2)
+            if i + 3 < N_RT:
+                exps(i + 3, 1)
+            second(i, 0)
+            second(i, 1)
+            if i > 0:
+                store(i - 1)
+        store(N_RT - 1)

@@ -175,7 +175,8 @@ def tile_multiscalegeometricattention_kernel(tc, x, positions, values, temperatu
         nc.vector.tensor_scalar_mul(out=nhp2[:, 0:4], in0=p2[:, 0:4], scalar1=-0.5)
 
         def block(j):
-            return dist[j // 16][:, :, (j % 16) * P : (j % 16 + 1) * P]
+            s = (j % 4) * 4 + (j // 4) % 4
+            return dist[j // 16][:, :, s * P : (s + 1) * P]
 
         def product(j, g):
             acols = slice(j * P, (j + 1) * P)
@@ -200,9 +201,10 @@ def tile_multiscalegeometricattention_kernel(tc, x, positions, values, temperatu
             )
 
         def clamp(c, part):
-            lo = (c % 4) * CHUNK + part * 2 * P
-            view = dist[c // 4][:, :, lo : lo + 2 * P]
-            nc.vector.tensor_scalar_min(out=view, in0=view, scalar1=0.0)
+            half = dist[c // 4][:].rearrange("p i (t c m) -> p i t c m", t=4, c=4)
+            for t in (2 * part, 2 * part + 1):
+                view = half[:, :, t, c % 4, :]
+                nc.vector.tensor_scalar_min(out=view, in0=view, scalar1=0.0)
 
         def root(j):
             nc.scalar.activation(out=block(j), in_=block(j), func=ACT.Sqrt, scale=m2a[:, j : j + 1])
@@ -283,16 +285,21 @@ def tile_multiscalegeometricattention_kernel(tc, x, positions, values, temperatu
             nc.vector.tensor_scalar_add(out=rinv[:, i : i + 1], in0=rsum[:, i : i + 1], scalar1=1e-8)
             nc.vector.reciprocal(out=rinv[:, i : i + 1], in_=rinv[:, i : i + 1])
             rb[i] = psum.tile([P, 512], F32, tag="bank", name="rb")
-            nc.tensor.matmul(
-                out=rb[i][:, 0:P], lhsT=rinv[:, i : i + 1].to_broadcast([P, P]), rhs=ident_f[:], start=True, stop=True
-            )
+            for c in range(4):
+                nc.tensor.matmul(
+                    out=rb[i][:, c * P : (c + 1) * P],
+                    lhsT=rinv[:, i : i + 1].to_broadcast([P, P]),
+                    rhs=ident_f[:],
+                    start=True,
+                    stop=True,
+                )
 
         def weights(i, h):
             gw[(i, h)] = grp.tile([P, 4 * CHUNK], BF16, tag="grouped", name="gw", align_bytes=64)
             nc.vector.tensor_tensor(
-                out=gw[(i, h)][:].rearrange("p (c m t) -> p c m t", c=4, t=4),
-                in0=dist[h][:, i, :].rearrange("p (c t m) -> p c m t", c=4, t=4),
-                in1=rb[i][:, 0:P].unsqueeze(1).unsqueeze(3).to_broadcast([P, 4, P, 4]),
+                out=gw[(i, h)][:].rearrange("p (b k t) -> p b t k", k=4, t=4),
+                in0=dist[h][:, i, :].rearrange("p (t b k) -> p b t k", t=4, k=4),
+                in1=rb[i][:].rearrange("p (b k) -> p b k", k=4).unsqueeze(2).to_broadcast([P, P, 4, 4]),
                 op=ALU.mult,
             )
 

@@ -1,3 +1,4 @@
+import math
 from contextlib import ExitStack
 
 import concourse.mybir as mybir
@@ -21,9 +22,10 @@ N_RT = ROWS // P
 N_CH = ANCH // CHUNK
 N_GR = ROWS // CHUNK
 
-REGROUP_ON_G = False
-VAL_LATE = 6
-HEAD_COPIES_V = True
+VAL_EARLY = 4
+SPREAD = 4
+LOWEST = -3.0e38
+SQRT_HALF = math.sqrt(0.5)
 
 FLOPS = 2 * 2 * ROWS * ANCH * D
 
@@ -60,10 +62,8 @@ def tile_multiscalegeometricattention_kernel(tc, x, positions, values, temperatu
         vc = const.tile([P, N_CH * D], U32, align_bytes=64)
         vs = const.tile([P, N_CH * D], U8, align_bytes=64)
         x2 = const.tile([P, N_RT], F32)
-        nhx2 = const.tile([P, N_RT], F32)
         p2 = const.tile([P, 4 * N_CH], F32)
-        nhp2 = const.tile([P, 4 * N_CH], F32)
-        nhx2b = const.tile([P, ROWS], F32)
+        hx2b = const.tile([P, ROWS], F32)
         rsum = const.tile([P, N_RT], F32)
         rinv = const.tile([P, N_RT], F32)
         junk_s = const.tile([P, D], BF16)
@@ -79,9 +79,12 @@ def tile_multiscalegeometricattention_kernel(tc, x, positions, values, temperatu
             nc.sync.dma_start(out=raw[:], in_=src.rearrange("(p i) d -> p i d", i=4))
             return raw
 
+        def square(raw, i, half_sum):
+            nc.scalar.activation(out=junk_s[:], in_=raw[:, i, :], func=ACT.Square, scale=SQRT_HALF, accum_out=half_sum)
+
         def squares(raw, sums):
             for i in range(4):
-                nc.scalar.activation(out=junk_s[:], in_=raw[:, i, :], func=ACT.Square, accum_out=sums[:, i : i + 1])
+                square(raw, i, sums[:, i : i + 1])
 
         def word_transposes(raw):
             words = raw[:].bitcast(F32)
@@ -116,16 +119,16 @@ def tile_multiscalegeometricattention_kernel(tc, x, positions, values, temperatu
                 t = 4 * g + i
                 nc.tensor.matmul(
                     out=bbank[:, i * P : (i + 1) * P],
-                    lhsT=nhx2[:, t : t + 1].to_broadcast([P, P]),
+                    lhsT=x2[:, t : t + 1].to_broadcast([P, P]),
                     rhs=ident_f[:],
                     start=True,
                     stop=True,
                 )
             return bbank
 
-        def regroup_values(raw):
+        def regroup_values(raw, on_gpsimd):
             grouped = grp.tile([P, 4 * D], BF16, tag="grouped", name="grouped", align_bytes=64)
-            if REGROUP_ON_G:
+            if on_gpsimd:
                 nc.gpsimd.tensor_scalar(
                     out=grouped[:].rearrange("p (d t) -> p d t", t=4),
                     in0=raw[:].rearrange("p t d -> p d t"),
@@ -147,7 +150,7 @@ def tile_multiscalegeometricattention_kernel(tc, x, positions, values, temperatu
         raw_p = {0: load(rawp, pos_chunk(0))}
         raw_x1 = load(rawp, xf[CHUNK : 2 * CHUNK, :])
         raw_p[1] = load(rawp, pos_chunk(1))
-        raw_v = {}
+        raw_v = {0: load(rawv, val_chunk(0)), 1: load(rawv, val_chunk(1))}
 
         nc.vector.scalar_tensor_tensor(out=tau[:], in0=temp_b[:], scalar=-1.0, in1=temp_b[:], op0=ALU.mult, op1=ALU.max)
         nc.vector.tensor_scalar(out=tau[:], in0=tau[:], scalar1=0.1, scalar2=0.05, op0=ALU.add, op1=ALU.mult)
@@ -155,24 +158,16 @@ def tile_multiscalegeometricattention_kernel(tc, x, positions, values, temperatu
         nc.vector.reciprocal(out=m2a[:], in_=m2a[:])
         nc.vector.tensor_scalar_mul(out=m2a[:], in0=m2a[:], scalar1=-2.0)
         squares(raw_x0, x2[:, 0:4])
-        g_x0 = copy_out(HEAD_COPIES_V, word_transposes(raw_x0))
+        g_x0 = copy_out(True, word_transposes(raw_x0))
         raw_p[2] = load(rawp, pos_chunk(2))
-        squares(raw_x1, x2[:, 4:8])
-        g_p0 = copy_out(HEAD_COPIES_V, word_transposes(raw_p[0]))
-        quantise(g_x0, xc[:, 0:CHUNK], xs[:, 0:CHUNK])
-        g_x1 = copy_out(HEAD_COPIES_V, word_transposes(raw_x1))
-        raw_p[3] = load(rawp, pos_chunk(3))
-        quantise(g_p0, pc[:, 0:CHUNK], ps[:, 0:CHUNK])
         squares(raw_p[0], p2[:, 0:4])
-        raw_v[0] = load(rawv, val_chunk(0))
-        raw_v[1] = load(rawv, val_chunk(1))
-        nc.vector.tensor_scalar_mul(out=nhx2[:], in0=x2[:], scalar1=-0.5)
+        g_p0 = copy_out(True, word_transposes(raw_p[0]))
+        quantise(g_x0, xc[:, 0:CHUNK], xs[:, 0:CHUNK])
         bb0 = spread_x2(0)
-        bb1 = spread_x2(1)
-        quantise(g_x1, xc[:, CHUNK : 2 * CHUNK], xs[:, CHUNK : 2 * CHUNK])
-        nc.vector.tensor_copy(out=nhx2b[:, 0:CHUNK], in_=bb0[:])
-        nc.vector.tensor_copy(out=nhx2b[:, CHUNK : 2 * CHUNK], in_=bb1[:])
-        nc.vector.tensor_scalar_mul(out=nhp2[:, 0:4], in0=p2[:, 0:4], scalar1=-0.5)
+        quantise(g_p0, pc[:, 0:CHUNK], ps[:, 0:CHUNK])
+        nc.vector.tensor_copy(out=hx2b[:, 0:CHUNK], in_=bb0[:])
+        squares(raw_x1, x2[:, 4:8])
+        banks_x1 = word_transposes(raw_x1)
 
         def block(j):
             s = (j % 4) * 4 + (j // 4) % 4
@@ -194,66 +189,69 @@ def tile_multiscalegeometricattention_kernel(tc, x, positions, values, temperatu
             nc.vector.scalar_tensor_tensor(
                 out=block(j)[:, 4 * g : 4 * g + 4, :],
                 in0=sbank[:].rearrange("p (i m) -> p i m", i=4),
-                scalar=nhp2[:, j : j + 1],
-                in1=nhx2b[:, cols].rearrange("p (i m) -> p i m", i=4),
-                op0=ALU.add,
-                op1=ALU.add,
+                scalar=p2[:, j : j + 1],
+                in1=hx2b[:, cols].rearrange("p (i m) -> p i m", i=4),
+                op0=ALU.subtract,
+                op1=ALU.subtract,
             )
 
-        def clamp(c, part):
-            half = dist[c // 4][:].rearrange("p i (t c m) -> p i t c m", t=4, c=4)
-            for t in (2 * part, 2 * part + 1):
-                view = half[:, :, t, c % 4, :]
-                nc.vector.tensor_scalar_min(out=view, in0=view, scalar1=0.0)
+        def clamp(j):
+            nc.gpsimd.tensor_scalar(
+                out=block(j), in0=block(j), scalar1=0.0, scalar2=LOWEST, op0=ALU.min, op1=ALU.max
+            )
 
         def root(j):
             nc.scalar.activation(out=block(j), in_=block(j), func=ACT.Sqrt, scale=m2a[:, j : j + 1])
 
         g_v = {}
 
-        def values_a(c):
-            g_v[c] = regroup_values(raw_v[c])
+        def values_a(c, on_gpsimd):
+            g_v[c] = regroup_values(raw_v[c], on_gpsimd)
             if c + 2 < N_CH:
                 raw_v[c + 2] = load(rawv, val_chunk(c + 2))
 
         def values_b(c):
             quantise(g_v[c], vc[:, c * D : (c + 1) * D], vs[:, c * D : (c + 1) * D])
 
-        n_early = N_CH - VAL_LATE
+        values_a(0, True)
+        values_a(1, True)
+        for j in range(4):
+            product(j, 0)
+        g_x1 = copy_out(True, banks_x1)
+        bb1 = spread_x2(1)
+        quantise(g_x1, xc[:, CHUNK : 2 * CHUNK], xs[:, CHUNK : 2 * CHUNK])
+        nc.vector.tensor_copy(out=hx2b[:, CHUNK : 2 * CHUNK], in_=bb1[:])
         for c in range(N_CH):
             nxt = c + 1
             if nxt < N_CH:
-                g_next = copy_out(False, word_transposes(raw_p[nxt]))
-                squares(raw_p[nxt], p2[:, 4 * nxt : 4 * nxt + 4])
-                if nxt + 3 < N_CH:
-                    raw_p[nxt + 3] = load(rawp, pos_chunk(nxt + 3))
+                banks = word_transposes(raw_p[nxt])
             for jj in range(4):
                 j = 4 * c + jj
-                product(j, 0)
+                if c > 0:
+                    product(j, 0)
                 product(j, 1)
-                if jj == 0 and c > 0:
-                    clamp(c - 1, 1)
+                clamp(j)
+                if j >= 2:
                     root(j - 2)
-                    root(j - 1)
-                if jj == 1 and c < n_early:
-                    values_a(c)
-                if jj == 2:
-                    clamp(c, 0)
-                    root(j - 2)
-                    root(j - 1)
-                    if nxt < N_CH:
+                if nxt < N_CH:
+                    square(raw_p[nxt], jj, p2[:, 4 * nxt + jj : 4 * nxt + jj + 1])
+                    if jj == 0:
+                        g_next = copy_out(True, banks)
+                    if jj == 2:
                         quantise(g_next, pc[:, nxt * CHUNK : (nxt + 1) * CHUNK], ps[:, nxt * CHUNK : (nxt + 1) * CHUNK])
-                        nc.vector.tensor_scalar_mul(
-                            out=nhp2[:, 4 * nxt : 4 * nxt + 4], in0=p2[:, 4 * nxt : 4 * nxt + 4], scalar1=-0.5
-                        )
-                if jj == 3 and c < n_early:
-                    values_b(c)
-        clamp(N_CH - 1, 1)
+            if nxt + 2 < N_CH:
+                raw_p[nxt + 2] = load(rawp, pos_chunk(nxt + 2))
+            if c in (1, 3):
+                values_b(c // 2)
+            if c in (2, 4):
+                values_a(c // 2 + 1, False)
+            if c in (5, 6):
+                values_b(c - 3)
         root(4 * N_CH - 2)
         root(4 * N_CH - 1)
-        for c in range(n_early, N_CH):
-            values_a(c)
-            if c > n_early:
+        for c in range(VAL_EARLY, N_CH):
+            values_a(c, False)
+            if c > VAL_EARLY:
                 values_b(c - 1)
         values_b(N_CH - 1)
 
@@ -285,7 +283,7 @@ def tile_multiscalegeometricattention_kernel(tc, x, positions, values, temperatu
             nc.vector.tensor_scalar_add(out=rinv[:, i : i + 1], in0=rsum[:, i : i + 1], scalar1=1e-8)
             nc.vector.reciprocal(out=rinv[:, i : i + 1], in_=rinv[:, i : i + 1])
             rb[i] = psum.tile([P, 512], F32, tag="bank", name="rb")
-            for c in range(4):
+            for c in range(SPREAD):
                 nc.tensor.matmul(
                     out=rb[i][:, c * P : (c + 1) * P],
                     lhsT=rinv[:, i : i + 1].to_broadcast([P, P]),
@@ -296,12 +294,15 @@ def tile_multiscalegeometricattention_kernel(tc, x, positions, values, temperatu
 
         def weights(i, h):
             gw[(i, h)] = grp.tile([P, 4 * CHUNK], BF16, tag="grouped", name="gw", align_bytes=64)
-            nc.vector.tensor_tensor(
-                out=gw[(i, h)][:].rearrange("p (b k t) -> p b t k", k=4, t=4),
-                in0=dist[h][:, i, :].rearrange("p (t b k) -> p b t k", t=4, k=4),
-                in1=rb[i][:].rearrange("p (b k) -> p b k", k=4).unsqueeze(2).to_broadcast([P, P, 4, 4]),
-                op=ALU.mult,
-            )
+            parts = 4 // SPREAD
+            n = CHUNK * SPREAD
+            for q in range(parts):
+                nc.vector.tensor_tensor(
+                    out=gw[(i, h)][:, q * n : (q + 1) * n].rearrange("p (b k t) -> p b t k", k=4, t=4),
+                    in0=dist[h][:, i, :].rearrange("p (t q b k) -> p q b t k", q=parts, t=4, k=4)[:, q],
+                    in1=rb[i][:, 0 : n // 4].rearrange("p (b k) -> p b k", k=4).unsqueeze(2).to_broadcast([P, n // 16, 4, 4]),
+                    op=ALU.mult,
+                )
 
         def second(i, h):
             wc = wcp.tile([P, CHUNK], U32, tag="wc", name="wc", align_bytes=64)

@@ -22,8 +22,7 @@ N_RT = ROWS // P
 N_CH = ANCH // CHUNK
 N_GR = ROWS // CHUNK
 
-VAL_EARLY = 4
-SPREAD = 4
+SPREAD = 2
 LOWEST = -3.0e38
 SQRT_HALF = math.sqrt(0.5)
 
@@ -37,8 +36,7 @@ def tile_multiscalegeometricattention_kernel(tc, x, positions, values, temperatu
 
     with ExitStack() as ctx:
         const = ctx.enter_context(tc.tile_pool(name="const", bufs=1))
-        rawp = ctx.enter_context(tc.tile_pool(name="rawp", bufs=4))
-        rawv = ctx.enter_context(tc.tile_pool(name="rawv", bufs=2))
+        rawp = ctx.enter_context(tc.tile_pool(name="rawp", bufs=6))
         grp = ctx.enter_context(tc.tile_pool(name="grp", bufs=4))
         wcp = ctx.enter_context(tc.tile_pool(name="wcp", bufs=3))
         outp = ctx.enter_context(tc.tile_pool(name="outp", bufs=2))
@@ -98,16 +96,13 @@ def tile_multiscalegeometricattention_kernel(tc, x, positions, values, temperatu
                 banks.append(bank)
             return banks
 
-        def copy_out(on_vector, banks):
+        def copy_out(banks):
             grouped = grp.tile([P, 4 * CHUNK], BF16, tag="grouped", name="grouped", align_bytes=64)
             gwords = grouped[:].bitcast(F32)
             for b in range(2):
                 dst = gwords[:, 512 * b : 512 * (b + 1)].rearrange("q (i m u) -> q i m u", i=2, u=2)
                 src = banks[b][:].rearrange("q (i u m) -> q i m u", i=2, u=2)
-                if on_vector:
-                    nc.vector.tensor_copy(out=dst, in_=src)
-                else:
-                    nc.scalar.copy(out=dst, in_=src)
+                nc.vector.tensor_copy(out=dst, in_=src)
             return grouped
 
         def quantise(grouped, codes, scales):
@@ -126,22 +121,12 @@ def tile_multiscalegeometricattention_kernel(tc, x, positions, values, temperatu
                 )
             return bbank
 
-        def regroup_values(raw, on_gpsimd):
+        def regroup_values(raw):
             grouped = grp.tile([P, 4 * D], BF16, tag="grouped", name="grouped", align_bytes=64)
-            if on_gpsimd:
-                nc.gpsimd.tensor_scalar(
-                    out=grouped[:].rearrange("p (d t) -> p d t", t=4),
-                    in0=raw[:].rearrange("p t d -> p d t"),
-                    scalar1=1.0,
-                    scalar2=0.0,
-                    op0=ALU.mult,
-                    op1=ALU.add,
-                )
-            else:
-                nc.vector.tensor_copy(
-                    out=grouped[:].rearrange("p (c i t) -> p c t i", i=4, t=4),
-                    in_=raw[:].rearrange("p t (c i) -> p c t i", i=4),
-                )
+            nc.vector.tensor_copy(
+                out=grouped[:].rearrange("p (c i t) -> p c t i", i=4, t=4),
+                in_=raw[:].rearrange("p t (c i) -> p c t i", i=4),
+            )
             return grouped
 
         pos_chunk = lambda c: positions[c * CHUNK : (c + 1) * CHUNK, :]
@@ -150,7 +135,6 @@ def tile_multiscalegeometricattention_kernel(tc, x, positions, values, temperatu
         raw_p = {0: load(rawp, pos_chunk(0))}
         raw_x1 = load(rawp, xf[CHUNK : 2 * CHUNK, :])
         raw_p[1] = load(rawp, pos_chunk(1))
-        raw_v = {0: load(rawv, val_chunk(0)), 1: load(rawv, val_chunk(1))}
 
         nc.vector.scalar_tensor_tensor(out=tau[:], in0=temp_b[:], scalar=-1.0, in1=temp_b[:], op0=ALU.mult, op1=ALU.max)
         nc.vector.tensor_scalar(out=tau[:], in0=tau[:], scalar1=0.1, scalar2=0.05, op0=ALU.add, op1=ALU.mult)
@@ -158,16 +142,18 @@ def tile_multiscalegeometricattention_kernel(tc, x, positions, values, temperatu
         nc.vector.reciprocal(out=m2a[:], in_=m2a[:])
         nc.vector.tensor_scalar_mul(out=m2a[:], in0=m2a[:], scalar1=-2.0)
         squares(raw_x0, x2[:, 0:4])
-        g_x0 = copy_out(True, word_transposes(raw_x0))
+        g_x0 = copy_out(word_transposes(raw_x0))
         raw_p[2] = load(rawp, pos_chunk(2))
+        raw_v = {}
         squares(raw_p[0], p2[:, 0:4])
-        g_p0 = copy_out(True, word_transposes(raw_p[0]))
+        g_p0 = copy_out(word_transposes(raw_p[0]))
         quantise(g_x0, xc[:, 0:CHUNK], xs[:, 0:CHUNK])
         bb0 = spread_x2(0)
         quantise(g_p0, pc[:, 0:CHUNK], ps[:, 0:CHUNK])
         nc.vector.tensor_copy(out=hx2b[:, 0:CHUNK], in_=bb0[:])
         squares(raw_x1, x2[:, 4:8])
         banks_x1 = word_transposes(raw_x1)
+        raw_p[3] = load(rawp, pos_chunk(3))
 
         def block(j):
             s = (j % 4) * 4 + (j // 4) % 4
@@ -195,63 +181,71 @@ def tile_multiscalegeometricattention_kernel(tc, x, positions, values, temperatu
                 op1=ALU.subtract,
             )
 
-        def clamp(j):
-            nc.gpsimd.tensor_scalar(
-                out=block(j), in0=block(j), scalar1=0.0, scalar2=LOWEST, op0=ALU.min, op1=ALU.max
-            )
+        def clamp(j, rows=slice(0, N_RT)):
+            view = block(j)[:, rows, :]
+            nc.gpsimd.tensor_scalar(out=view, in0=view, scalar1=0.0, scalar2=LOWEST, op0=ALU.min, op1=ALU.max)
 
-        def root(j):
-            nc.scalar.activation(out=block(j), in_=block(j), func=ACT.Sqrt, scale=m2a[:, j : j + 1])
+        def root(j, rows=slice(0, N_RT)):
+            view = block(j)[:, rows, :]
+            nc.scalar.activation(out=view, in_=view, func=ACT.Sqrt, scale=m2a[:, j : j + 1])
 
         g_v = {}
 
-        def values_a(c, on_gpsimd):
-            g_v[c] = regroup_values(raw_v[c], on_gpsimd)
-            if c + 2 < N_CH:
-                raw_v[c + 2] = load(rawv, val_chunk(c + 2))
+        def values_a(c):
+            g_v[c] = regroup_values(raw_v[c])
+            if c + 3 < N_CH:
+                raw_v[c + 3] = load(rawp, val_chunk(c + 3))
 
         def values_b(c):
             quantise(g_v[c], vc[:, c * D : (c + 1) * D], vs[:, c * D : (c + 1) * D])
 
-        values_a(0, True)
-        values_a(1, True)
+        first, second_half = slice(0, 4), slice(4, 8)
+        banks = word_transposes(raw_p[1])
         for j in range(4):
             product(j, 0)
-        g_x1 = copy_out(True, banks_x1)
-        bb1 = spread_x2(1)
-        quantise(g_x1, xc[:, CHUNK : 2 * CHUNK], xs[:, CHUNK : 2 * CHUNK])
-        nc.vector.tensor_copy(out=hx2b[:, CHUNK : 2 * CHUNK], in_=bb1[:])
-        for c in range(N_CH):
+            clamp(j, first)
+            if j == 0:
+                g_x1 = copy_out(banks_x1)
+            if j == 1:
+                quantise(g_x1, xc[:, CHUNK : 2 * CHUNK], xs[:, CHUNK : 2 * CHUNK])
+            if j == 2:
+                bb1 = spread_x2(1)
+                nc.vector.tensor_copy(out=hx2b[:, CHUNK : 2 * CHUNK], in_=bb1[:])
+        g_next = copy_out(banks)
+        squares(raw_p[1], p2[:, 4:8])
+        for j in range(4):
+            root(j, first)
+        quantise(g_next, pc[:, CHUNK : 2 * CHUNK], ps[:, CHUNK : 2 * CHUNK])
+        for j in range(4):
+            product(j, 1)
+            clamp(j, second_half)
+            root(j, second_half)
+        for c in range(1, N_CH):
             nxt = c + 1
             if nxt < N_CH:
                 banks = word_transposes(raw_p[nxt])
             for jj in range(4):
                 j = 4 * c + jj
-                if c > 0:
-                    product(j, 0)
+                product(j, 0)
                 product(j, 1)
                 clamp(j)
-                if j >= 2:
+                if j >= 6:
                     root(j - 2)
                 if nxt < N_CH:
                     square(raw_p[nxt], jj, p2[:, 4 * nxt + jj : 4 * nxt + jj + 1])
                     if jj == 0:
-                        g_next = copy_out(True, banks)
+                        g_next = copy_out(banks)
                     if jj == 2:
                         quantise(g_next, pc[:, nxt * CHUNK : (nxt + 1) * CHUNK], ps[:, nxt * CHUNK : (nxt + 1) * CHUNK])
             if nxt + 2 < N_CH:
                 raw_p[nxt + 2] = load(rawp, pos_chunk(nxt + 2))
-            if c in (1, 3):
-                values_b(c // 2)
-            if c in (2, 4):
-                values_a(c // 2 + 1, False)
-            if c in (5, 6):
-                values_b(c - 3)
+            else:
+                raw_v[nxt + 2 - N_CH] = load(rawp, val_chunk(nxt + 2 - N_CH))
         root(4 * N_CH - 2)
         root(4 * N_CH - 1)
-        for c in range(VAL_EARLY, N_CH):
-            values_a(c, False)
-            if c > VAL_EARLY:
+        for c in range(N_CH):
+            values_a(c)
+            if c > 0:
                 values_b(c - 1)
         values_b(N_CH - 1)
 

@@ -22,7 +22,7 @@ N_RT = ROWS // P
 N_CH = ANCH // CHUNK
 N_GR = ROWS // CHUNK
 
-SPREAD = 2
+CLAMPS_ON_G = 29
 LOWEST = -3.0e38
 SQRT_HALF = math.sqrt(0.5)
 
@@ -112,13 +112,7 @@ def tile_multiscalegeometricattention_kernel(tc, x, positions, values, temperatu
             bbank = psum.tile([P, 512], F32, tag="bank", name="bbank")
             for i in range(4):
                 t = 4 * g + i
-                nc.tensor.matmul(
-                    out=bbank[:, i * P : (i + 1) * P],
-                    lhsT=x2[:, t : t + 1].to_broadcast([P, P]),
-                    rhs=ident_f[:],
-                    start=True,
-                    stop=True,
-                )
+                nc.tensor.transpose(bbank[:, i * P : (i + 1) * P], x2[:, t : t + 1].to_broadcast([P, P]), ident_f[:])
             return bbank
 
         def regroup_values(raw):
@@ -154,6 +148,7 @@ def tile_multiscalegeometricattention_kernel(tc, x, positions, values, temperatu
         squares(raw_x1, x2[:, 4:8])
         banks_x1 = word_transposes(raw_x1)
         raw_p[3] = load(rawp, pos_chunk(3))
+        raw_p[4] = load(rawp, pos_chunk(4))
 
         def block(j):
             s = (j % 4) * 4 + (j // 4) % 4
@@ -183,7 +178,10 @@ def tile_multiscalegeometricattention_kernel(tc, x, positions, values, temperatu
 
         def clamp(j, rows=slice(0, N_RT)):
             view = block(j)[:, rows, :]
-            nc.gpsimd.tensor_scalar(out=view, in0=view, scalar1=0.0, scalar2=LOWEST, op0=ALU.min, op1=ALU.max)
+            if j >= CLAMPS_ON_G:
+                nc.vector.tensor_scalar_min(out=view, in0=view, scalar1=0.0)
+            else:
+                nc.gpsimd.tensor_scalar(out=view, in0=view, scalar1=0.0, scalar2=LOWEST, op0=ALU.min, op1=ALU.max)
 
         def root(j, rows=slice(0, N_RT)):
             view = block(j)[:, rows, :]
@@ -193,13 +191,14 @@ def tile_multiscalegeometricattention_kernel(tc, x, positions, values, temperatu
 
         def values_a(c):
             g_v[c] = regroup_values(raw_v[c])
-            if c + 3 < N_CH:
-                raw_v[c + 3] = load(rawp, val_chunk(c + 3))
+            if c + 4 < N_CH:
+                raw_v[c + 4] = load(rawp, val_chunk(c + 4))
 
         def values_b(c):
             quantise(g_v[c], vc[:, c * D : (c + 1) * D], vs[:, c * D : (c + 1) * D])
 
         first, second_half = slice(0, 4), slice(4, 8)
+        g_p = {}
         banks = word_transposes(raw_p[1])
         for j in range(4):
             product(j, 0)
@@ -211,19 +210,22 @@ def tile_multiscalegeometricattention_kernel(tc, x, positions, values, temperatu
             if j == 2:
                 bb1 = spread_x2(1)
                 nc.vector.tensor_copy(out=hx2b[:, CHUNK : 2 * CHUNK], in_=bb1[:])
-        g_next = copy_out(banks)
+        g_p[1] = copy_out(banks)
         squares(raw_p[1], p2[:, 4:8])
         for j in range(4):
             root(j, first)
-        quantise(g_next, pc[:, CHUNK : 2 * CHUNK], ps[:, CHUNK : 2 * CHUNK])
+        quantise(g_p[1], pc[:, CHUNK : 2 * CHUNK], ps[:, CHUNK : 2 * CHUNK])
         for j in range(4):
             product(j, 1)
             clamp(j, second_half)
             root(j, second_half)
+            if j == 0:
+                banks = word_transposes(raw_p[2])
+            if j == 1:
+                g_p[2] = copy_out(banks)
         for c in range(1, N_CH):
-            nxt = c + 1
-            if nxt < N_CH:
-                banks = word_transposes(raw_p[nxt])
+            n1 = c + 1
+            n2 = c + 2
             for jj in range(4):
                 j = 4 * c + jj
                 product(j, 0)
@@ -231,16 +233,19 @@ def tile_multiscalegeometricattention_kernel(tc, x, positions, values, temperatu
                 clamp(j)
                 if j >= 6:
                     root(j - 2)
-                if nxt < N_CH:
-                    square(raw_p[nxt], jj, p2[:, 4 * nxt + jj : 4 * nxt + jj + 1])
-                    if jj == 0:
-                        g_next = copy_out(banks)
+                if n1 < N_CH:
+                    square(raw_p[n1], jj, p2[:, 4 * n1 + jj : 4 * n1 + jj + 1])
                     if jj == 2:
-                        quantise(g_next, pc[:, nxt * CHUNK : (nxt + 1) * CHUNK], ps[:, nxt * CHUNK : (nxt + 1) * CHUNK])
-            if nxt + 2 < N_CH:
-                raw_p[nxt + 2] = load(rawp, pos_chunk(nxt + 2))
-            else:
-                raw_v[nxt + 2 - N_CH] = load(rawp, val_chunk(nxt + 2 - N_CH))
+                        quantise(g_p[n1], pc[:, n1 * CHUNK : (n1 + 1) * CHUNK], ps[:, n1 * CHUNK : (n1 + 1) * CHUNK])
+                if n2 < N_CH:
+                    if jj == 0:
+                        banks = word_transposes(raw_p[n2])
+                    if jj == 1:
+                        g_p[n2] = copy_out(banks)
+            if c + 4 < N_CH:
+                raw_p[c + 4] = load(rawp, pos_chunk(c + 4))
+            elif c + 4 - N_CH < 4:
+                raw_v[c + 4 - N_CH] = load(rawp, val_chunk(c + 4 - N_CH))
         root(4 * N_CH - 2)
         root(4 * N_CH - 1)
         for c in range(N_CH):
@@ -271,32 +276,22 @@ def tile_multiscalegeometricattention_kernel(tc, x, positions, values, temperatu
                 )
 
         def row_sum(i):
-            nc.scalar.activation(out=junk_r[:], in_=acc[i][:, 0:P], func=ACT.Identity, accum_out=rsum[:, i : i + 1])
+            nc.scalar.activation(out=junk_r[:], in_=acc[i][:, 0:P], func=ACT.Identity, bias=1e-8 / P, accum_out=rsum[:, i : i + 1])
 
         def inverse(i):
-            nc.vector.tensor_scalar_add(out=rinv[:, i : i + 1], in0=rsum[:, i : i + 1], scalar1=1e-8)
-            nc.vector.reciprocal(out=rinv[:, i : i + 1], in_=rinv[:, i : i + 1])
+            nc.vector.reciprocal(out=rinv[:, i : i + 1], in_=rsum[:, i : i + 1])
             rb[i] = psum.tile([P, 512], F32, tag="bank", name="rb")
-            for c in range(SPREAD):
-                nc.tensor.matmul(
-                    out=rb[i][:, c * P : (c + 1) * P],
-                    lhsT=rinv[:, i : i + 1].to_broadcast([P, P]),
-                    rhs=ident_f[:],
-                    start=True,
-                    stop=True,
-                )
+            for c in range(4):
+                nc.tensor.transpose(rb[i][:, c * P : (c + 1) * P], rinv[:, i : i + 1].to_broadcast([P, P]), ident_f[:])
 
         def weights(i, h):
             gw[(i, h)] = grp.tile([P, 4 * CHUNK], BF16, tag="grouped", name="gw", align_bytes=64)
-            parts = 4 // SPREAD
-            n = CHUNK * SPREAD
-            for q in range(parts):
-                nc.vector.tensor_tensor(
-                    out=gw[(i, h)][:, q * n : (q + 1) * n].rearrange("p (b k t) -> p b t k", k=4, t=4),
-                    in0=dist[h][:, i, :].rearrange("p (t q b k) -> p q b t k", q=parts, t=4, k=4)[:, q],
-                    in1=rb[i][:, 0 : n // 4].rearrange("p (b k) -> p b k", k=4).unsqueeze(2).to_broadcast([P, n // 16, 4, 4]),
-                    op=ALU.mult,
-                )
+            nc.vector.tensor_tensor(
+                out=gw[(i, h)][:].rearrange("p (b k t) -> p b t k", k=4, t=4),
+                in0=dist[h][:, i, :].rearrange("p (t b k) -> p b t k", t=4, k=4),
+                in1=rb[i][:].rearrange("p (b k) -> p b k", k=4).unsqueeze(2).to_broadcast([P, P, 4, 4]),
+                op=ALU.mult,
+            )
 
         def second(i, h):
             wc = wcp.tile([P, CHUNK], U32, tag="wc", name="wc", align_bytes=64)

@@ -23,6 +23,7 @@ N_CH = ANCH // CHUNK
 N_GR = ROWS // CHUNK
 
 CLAMPS_ON_G = 29
+SHARE = 1
 LOWEST = -3.0e38
 SQRT_HALF = math.sqrt(0.5)
 
@@ -39,6 +40,7 @@ def tile_multiscalegeometricattention_kernel(tc, x, positions, values, temperatu
         rawp = ctx.enter_context(tc.tile_pool(name="rawp", bufs=6))
         grp = ctx.enter_context(tc.tile_pool(name="grp", bufs=4))
         wcp = ctx.enter_context(tc.tile_pool(name="wcp", bufs=3))
+        rbp = ctx.enter_context(tc.tile_pool(name="rbp", bufs=2))
         outp = ctx.enter_context(tc.tile_pool(name="outp", bufs=2))
         psum = ctx.enter_context(tc.psum_pool(name="psum", bufs=8))
         ctx.enter_context(tc.manual_schedule())
@@ -235,12 +237,12 @@ def tile_multiscalegeometricattention_kernel(tc, x, positions, values, temperatu
                     root(j - 2)
                 if n1 < N_CH:
                     square(raw_p[n1], jj, p2[:, 4 * n1 + jj : 4 * n1 + jj + 1])
-                    if jj == 2:
+                    if jj == 0:
                         quantise(g_p[n1], pc[:, n1 * CHUNK : (n1 + 1) * CHUNK], ps[:, n1 * CHUNK : (n1 + 1) * CHUNK])
                 if n2 < N_CH:
-                    if jj == 0:
+                    if jj == 2:
                         banks = word_transposes(raw_p[n2])
-                    if jj == 1:
+                    if jj == 3:
                         g_p[n2] = copy_out(banks)
             if c + 4 < N_CH:
                 raw_p[c + 4] = load(rawp, pos_chunk(c + 4))
@@ -248,12 +250,6 @@ def tile_multiscalegeometricattention_kernel(tc, x, positions, values, temperatu
                 raw_v[c + 4 - N_CH] = load(rawp, val_chunk(c + 4 - N_CH))
         root(4 * N_CH - 2)
         root(4 * N_CH - 1)
-        for c in range(N_CH):
-            values_a(c)
-            if c > 0:
-                values_b(c - 1)
-        values_b(N_CH - 1)
-
         acc = {}
         rb = {}
         gw = {}
@@ -284,14 +280,22 @@ def tile_multiscalegeometricattention_kernel(tc, x, positions, values, temperatu
             for c in range(4):
                 nc.tensor.transpose(rb[i][:, c * P : (c + 1) * P], rinv[:, i : i + 1].to_broadcast([P, P]), ident_f[:])
 
-        def weights(i, h):
-            gw[(i, h)] = grp.tile([P, 4 * CHUNK], BF16, tag="grouped", name="gw", align_bytes=64)
-            nc.vector.tensor_tensor(
-                out=gw[(i, h)][:].rearrange("p (b k t) -> p b t k", k=4, t=4),
-                in0=dist[h][:, i, :].rearrange("p (t b k) -> p b t k", t=4, k=4),
-                in1=rb[i][:].rearrange("p (b k) -> p b k", k=4).unsqueeze(2).to_broadcast([P, P, 4, 4]),
+        def multiply(engine, i, h, lo, hi, factor):
+            engine.tensor_tensor(
+                out=gw[(i, h)][:, lo * CHUNK : hi * CHUNK].rearrange("p (b k t) -> p b t k", k=4, t=4),
+                in0=dist[h][:, i, :].rearrange("p (t b k) -> p b t k", t=4, k=4)[:, lo * 32 : hi * 32],
+                in1=factor.rearrange("p (b k) -> p b k", k=4).unsqueeze(2).to_broadcast([P, (hi - lo) * 32, 4, 4]),
                 op=ALU.mult,
             )
+
+        def weights(i):
+            for h in range(2):
+                gw[(i, h)] = grp.tile([P, 4 * CHUNK], BF16, tag="grouped", name="gw", align_bytes=64)
+            rbs = rbp.tile([P, SHARE * P], F32, tag="rbs", name="rbs")
+            nc.vector.tensor_copy(out=rbs[:], in_=rb[i][:, 0 : SHARE * P])
+            multiply(nc.gpsimd, i, 1, 4 - SHARE, 4, rbs[:])
+            multiply(nc.vector, i, 0, 0, 4, rb[i][:])
+            multiply(nc.vector, i, 1, 0, 4 - SHARE, rb[i][:, 0 : (4 - SHARE) * P])
 
         def second(i, h):
             wc = wcp.tile([P, CHUNK], U32, tag="wc", name="wc", align_bytes=64)
@@ -322,15 +326,22 @@ def tile_multiscalegeometricattention_kernel(tc, x, positions, values, temperatu
                 partial_sums(i, h)
 
         exp_tile(0)
+        exps(1, 0)
         row_sum(0)
+        for c in range(N_CH):
+            values_a(c)
+            if c > 0:
+                values_b(c - 1)
         inverse(0)
-        exp_tile(1)
+        values_b(N_CH - 1)
+        partial_sums(1, 0)
+        exps(1, 1)
+        partial_sums(1, 1)
         exps(2, 0)
         row_sum(1)
         exps(2, 1)
         for i in range(N_RT):
-            weights(i, 0)
-            weights(i, 1)
+            weights(i)
             if i + 1 < N_RT:
                 inverse(i + 1)
             if i + 2 < N_RT:

@@ -23,7 +23,7 @@ N_CH = ANCH // CHUNK
 N_GR = ROWS // CHUNK
 
 CLAMPS_ON_G = 29
-SHARE = 1
+SHARE = 2
 LOWEST = -3.0e38
 SQRT_HALF = math.sqrt(0.5)
 
@@ -280,8 +280,18 @@ def tile_multiscalegeometricattention_kernel(tc, x, positions, values, temperatu
             for c in range(4):
                 nc.tensor.transpose(rb[i][:, c * P : (c + 1) * P], rinv[:, i : i + 1].to_broadcast([P, P]), ident_f[:])
 
-        def multiply(engine, i, h, lo, hi, factor):
-            engine.tensor_tensor(
+        def multiply_on_gpsimd(i, h, lo, factor):
+            n = 4 - lo
+            nc.gpsimd.tensor_tensor(
+                out=gw[(i, h)][:, lo * CHUNK :].rearrange("p (c m t) -> p c m t", c=n, t=4),
+                in0=dist[h][:, i, :].rearrange("p (t c m) -> p c m t", t=4, c=4)[:, lo:4],
+                in1=factor.unsqueeze(1).unsqueeze(3).to_broadcast([P, n, P, 4]),
+                op=ALU.mult,
+            )
+
+        def multiply(i, h, lo, hi):
+            factor = rb[i][:, 0 : (hi - lo) * P]
+            nc.vector.tensor_tensor(
                 out=gw[(i, h)][:, lo * CHUNK : hi * CHUNK].rearrange("p (b k t) -> p b t k", k=4, t=4),
                 in0=dist[h][:, i, :].rearrange("p (t b k) -> p b t k", t=4, k=4)[:, lo * 32 : hi * 32],
                 in1=factor.rearrange("p (b k) -> p b k", k=4).unsqueeze(2).to_broadcast([P, (hi - lo) * 32, 4, 4]),
@@ -291,11 +301,16 @@ def tile_multiscalegeometricattention_kernel(tc, x, positions, values, temperatu
         def weights(i):
             for h in range(2):
                 gw[(i, h)] = grp.tile([P, 4 * CHUNK], BF16, tag="grouped", name="gw", align_bytes=64)
-            rbs = rbp.tile([P, SHARE * P], F32, tag="rbs", name="rbs")
-            nc.vector.tensor_copy(out=rbs[:], in_=rb[i][:, 0 : SHARE * P])
-            multiply(nc.gpsimd, i, 1, 4 - SHARE, 4, rbs[:])
-            multiply(nc.vector, i, 0, 0, 4, rb[i][:])
-            multiply(nc.vector, i, 1, 0, 4 - SHARE, rb[i][:, 0 : (4 - SHARE) * P])
+            rbs = rbp.tile([P, P], F32, tag="rbs", name="rbs")
+            nc.vector.tensor_copy(out=rbs[:], in_=rb[i][:, 0:P])
+            multiply_on_gpsimd(i, 1, 4 - SHARE, rbs[:])
+            multiply(i, 0, 0, 4)
+            if i < N_RT - 1:
+                multiply(i, 1, 0, 4 - SHARE)
+            else:
+                multiply(i, 1, 0, 1)
+                second(i, 0)
+                multiply(i, 1, 1, 4 - SHARE)
 
         def second(i, h):
             wc = wcp.tile([P, CHUNK], U32, tag="wc", name="wc", align_bytes=64)
@@ -317,8 +332,15 @@ def tile_multiscalegeometricattention_kernel(tc, x, positions, values, temperatu
 
         def store(i):
             ost = outp.tile([P, D], F32, tag="ost", name="ost")
-            nc.scalar.copy(out=ost[:], in_=obank[i][:])
-            nc.sync.dma_start(out=of[i // 4, i % 4], in_=ost[:])
+            if i < N_RT - 1:
+                nc.scalar.copy(out=ost[:], in_=obank[i][:])
+                nc.sync.dma_start(out=of[i // 4, i % 4], in_=ost[:])
+            else:
+                w = D // 2
+                nc.scalar.copy(out=ost[:, 0:w], in_=obank[i][:, 0:w])
+                nc.vector.tensor_copy(out=ost[:, w:D], in_=obank[i][:, w:D])
+                nc.sync.dma_start(out=of[i // 4, i % 4, :, 0:w], in_=ost[:, 0:w])
+                nc.sync.dma_start(out=of[i // 4, i % 4, :, w:D], in_=ost[:, w:D])
 
         def exp_tile(i):
             for h in range(2):
@@ -353,7 +375,8 @@ def tile_multiscalegeometricattention_kernel(tc, x, positions, values, temperatu
                 row_sum(i + 2)
             if i + 3 < N_RT:
                 exps(i + 3, 1)
-            second(i, 0)
+            if i < N_RT - 1:
+                second(i, 0)
             second(i, 1)
             if i > 0:
                 store(i - 1)

import math
from contextlib import ExitStack

import concourse.mybir as mybir
from concourse.masks import make_identity

F32 = mybir.dt.float32
BF16 = mybir.dt.bfloat16
U32 = mybir.dt.uint32
U8 = mybir.dt.uint8
FP8X4 = mybir.dt.float8_e4m3fn_x4
ALU = mybir.AluOpType
ACT = mybir.ActivationFunctionType

P = 128
D = 512
ROWS = 1024
ANCH = 4096
CHUNK = 512
HALF = 2048
N_RT = ROWS // P
N_CH = ANCH // CHUNK
N_GR = ROWS // CHUNK

CLAMPS_ON_G = 29
SHARE = 2
LOWEST = -3.0e38
SQRT_HALF = math.sqrt(0.5)

FLOPS = 2 * 2 * ROWS * ANCH * D


def tile_multiscalegeometricattention_kernel(tc, x, positions, values, temperature, out):
    nc = tc.nc
    xf = x.flatten_outer_dims()
    of = out.flatten_outer_dims().rearrange("(g m i) d -> g i m d", g=N_GR, i=4)

    with ExitStack() as ctx:
        const = ctx.enter_context(tc.tile_pool(name="const", bufs=1))
        rawp = ctx.enter_context(tc.tile_pool(name="rawp", bufs=6))
        grp = ctx.enter_context(tc.tile_pool(name="grp", bufs=4))
        wcp = ctx.enter_context(tc.tile_pool(name="wcp", bufs=3))
        rbp = ctx.enter_context(tc.tile_pool(name="rbp", bufs=2))
        outp = ctx.enter_context(tc.tile_pool(name="outp", bufs=2))
        psum = ctx.enter_context(tc.psum_pool(name="psum", bufs=8))
        ctx.enter_context(tc.manual_schedule())

        temp_b = const.tile([P, 4 * N_CH], BF16)
        nc.scalar.dma_start(
            out=temp_b[:].rearrange("p (c t) -> p c t", t=4), in_=temperature.rearrange("(c p t) -> p c t", p=P, t=4)
        )
        warm = const.tile([P, 1], F32)
        nc.vector.memset(warm[:], 1.0)
        nc.scalar.activation(out=warm[:], in_=warm[:], func=ACT.Sqrt)
        ident_f = const.tile([P, P], F32)
        make_identity(nc, ident_f[:])

        xc = const.tile([P, ROWS], U32, align_bytes=64)
        xs = const.tile([P, ROWS], U8, align_bytes=64)
        pc = const.tile([P, ANCH], U32, align_bytes=64)
        ps = const.tile([P, ANCH], U8, align_bytes=64)
        vc = const.tile([P, N_CH * D], U32, align_bytes=64)
        vs = const.tile([P, N_CH * D], U8, align_bytes=64)
        x2 = const.tile([P, N_RT], F32)
        p2 = const.tile([P, 4 * N_CH], F32)
        hx2b = const.tile([P, ROWS], F32)
        rsum = const.tile([P, N_RT], F32)
        rinv = const.tile([P, N_RT], F32)
        junk_s = const.tile([P, D], BF16)
        junk_r = const.tile([P, P], F32)
        tau = const.tile([P, 4 * N_CH], F32)
        m2a = const.tile([P, 4 * N_CH], F32)
        dist = []
        for h in range(2):
            dist.append(const.tile([P, N_RT, HALF], F32, name="dist%d" % h))

        def load(pool, src):
            raw = pool.tile([P, 4, D], BF16, tag="raw", name="raw")
            nc.sync.dma_start(out=raw[:], in_=src.rearrange("(p i) d -> p i d", i=4))
            return raw

        def square(raw, i, half_sum):
            nc.scalar.activation(out=junk_s[:], in_=raw[:, i, :], func=ACT.Square, scale=SQRT_HALF, accum_out=half_sum)

        def squares(raw, sums):
            for i in range(4):
                square(raw, i, sums[:, i : i + 1])

        def word_transposes(raw):
            words = raw[:].bitcast(F32)
            banks = []
            for b in range(2):
                bank = psum.tile([P, 512], F32, tag="bank", name="wbank")
                for ii in range(2):
                    for u in range(2):
                        s = 2 * ii + u
                        nc.tensor.transpose(bank[:, s * P : (s + 1) * P], words[:, 2 * b + ii, u * P : (u + 1) * P], ident_f[:])
                banks.append(bank)
            return banks

        def copy_out(banks):
            grouped = grp.tile([P, 4 * CHUNK], BF16, tag="grouped", name="grouped", align_bytes=64)
            gwords = grouped[:].bitcast(F32)
            for b in range(2):
                dst = gwords[:, 512 * b : 512 * (b + 1)].rearrange("q (i m u) -> q i m u", i=2, u=2)
                src = banks[b][:].rearrange("q (i u m) -> q i m u", i=2, u=2)
                nc.vector.tensor_copy(out=dst, in_=src)
            return grouped

        def quantise(grouped, codes, scales):
            nc.vector.quantize_mx(out=codes.bitcast(FP8X4), scales=scales, in_=grouped[:])

        def spread_x2(g):
            bbank = psum.tile([P, 512], F32, tag="bank", name="bbank")
            for i in range(4):
                t = 4 * g + i
                nc.tensor.transpose(bbank[:, i * P : (i + 1) * P], x2[:, t : t + 1].to_broadcast([P, P]), ident_f[:])
            return bbank

        def regroup_values(raw):
            grouped = grp.tile([P, 4 * D], BF16, tag="grouped", name="grouped", align_bytes=64)
            nc.vector.tensor_copy(
                out=grouped[:].rearrange("p (c i t) -> p c t i", i=4, t=4),
                in_=raw[:].rearrange("p t (c i) -> p c t i", i=4),
            )
            return grouped

        pos_chunk = lambda c: positions[c * CHUNK : (c + 1) * CHUNK, :]
        val_chunk = lambda c: values[c * CHUNK : (c + 1) * CHUNK, :]
        raw_x0 = load(rawp, xf[0:CHUNK, :])
        raw_p = {0: load(rawp, pos_chunk(0))}
        raw_x1 = load(rawp, xf[CHUNK : 2 * CHUNK, :])
        raw_p[1] = load(rawp, pos_chunk(1))

        nc.vector.scalar_tensor_tensor(out=tau[:], in0=temp_b[:], scalar=-1.0, in1=temp_b[:], op0=ALU.mult, op1=ALU.max)
        nc.vector.tensor_scalar(out=tau[:], in0=tau[:], scalar1=0.1, scalar2=0.05, op0=ALU.add, op1=ALU.mult)
        nc.vector.tensor_tensor(out=m2a[:], in0=tau[:], in1=tau[:], op=ALU.mult)
        nc.vector.reciprocal(out=m2a[:], in_=m2a[:])
        nc.vector.tensor_scalar_mul(out=m2a[:], in0=m2a[:], scalar1=-2.0)
        squares(raw_x0, x2[:, 0:4])
        g_x0 = copy_out(word_transposes(raw_x0))
        raw_p[2] = load(rawp, pos_chunk(2))
        raw_v = {}
        squares(raw_p[0], p2[:, 0:4])
        g_p0 = copy_out(word_transposes(raw_p[0]))
        quantise(g_x0, xc[:, 0:CHUNK], xs[:, 0:CHUNK])
        bb0 = spread_x2(0)
        quantise(g_p0, pc[:, 0:CHUNK], ps[:, 0:CHUNK])
        nc.vector.tensor_copy(out=hx2b[:, 0:CHUNK], in_=bb0[:])
        squares(raw_x1, x2[:, 4:8])
        banks_x1 = word_transposes(raw_x1)
        raw_p[3] = load(rawp, pos_chunk(3))
        raw_p[4] = load(rawp, pos_chunk(4))

        def block(j):
            s = (j % 4) * 4 + (j // 4) % 4
            return dist[j // 16][:, :, s * P : (s + 1) * P]

        def product(j, g):
            acols = slice(j * P, (j + 1) * P)
            cols = slice(g * CHUNK, (g + 1) * CHUNK)
            sbank = psum.tile([P, CHUNK], F32, tag="bank", name="sbank")
            nc.tensor.matmul_mx(
                out=sbank[:],
                lhsT=pc[:, acols].bitcast(FP8X4),
                lhsT_scale=ps[:, acols],
                rhs=xc[:, cols].bitcast(FP8X4),
                rhs_scale=xs[:, cols],
                start=True,
                stop=True,
            )
            nc.vector.scalar_tensor_tensor(
                out=block(j)[:, 4 * g : 4 * g + 4, :],
                in0=sbank[:].rearrange("p (i m) -> p i m", i=4),
                scalar=p2[:, j : j + 1],
                in1=hx2b[:, cols].rearrange("p (i m) -> p i m", i=4),
                op0=ALU.subtract,
                op1=ALU.subtract,
            )

        def clamp(j, rows=slice(0, N_RT)):
            view = block(j)[:, rows, :]
            if j >= CLAMPS_ON_G:
                nc.vector.tensor_scalar_min(out=view, in0=view, scalar1=0.0)
            else:
                nc.gpsimd.tensor_scalar(out=view, in0=view, scalar1=0.0, scalar2=LOWEST, op0=ALU.min, op1=ALU.max)

        def root(j, rows=slice(0, N_RT)):
            view = block(j)[:, rows, :]
            nc.scalar.activation(out=view, in_=view, func=ACT.Sqrt, scale=m2a[:, j : j + 1])

        g_v = {}

        def values_a(c):
            g_v[c] = regroup_values(raw_v[c])
            if c + 4 < N_CH:
                raw_v[c + 4] = load(rawp, val_chunk(c + 4))

        def values_b(c):
            quantise(g_v[c], vc[:, c * D : (c + 1) * D], vs[:, c * D : (c + 1) * D])

        first, second_half = slice(0, 4), slice(4, 8)
        g_p = {}
        banks = word_transposes(raw_p[1])
        for j in range(4):
            product(j, 0)
            clamp(j, first)
            if j == 0:
                g_x1 = copy_out(banks_x1)
            if j == 1:
                quantise(g_x1, xc[:, CHUNK : 2 * CHUNK], xs[:, CHUNK : 2 * CHUNK])
            if j == 2:
                bb1 = spread_x2(1)
                nc.vector.tensor_copy(out=hx2b[:, CHUNK : 2 * CHUNK], in_=bb1[:])
        g_p[1] = copy_out(banks)
        squares(raw_p[1], p2[:, 4:8])
        for j in range(4):
            root(j, first)
        quantise(g_p[1], pc[:, CHUNK : 2 * CHUNK], ps[:, CHUNK : 2 * CHUNK])
        for j in range(4):
            product(j, 1)
            clamp(j, second_half)
            root(j, second_half)
            if j == 0:
                banks = word_transposes(raw_p[2])
            if j == 1:
                g_p[2] = copy_out(banks)
        for c in range(1, N_CH):
            n1 = c + 1
            n2 = c + 2
            for jj in range(4):
                j = 4 * c + jj
                product(j, 0)
                product(j, 1)
                clamp(j)
                if j >= 6:
                    root(j - 2)
                if n1 < N_CH:
                    square(raw_p[n1], jj, p2[:, 4 * n1 + jj : 4 * n1 + jj + 1])
                    if jj == 0:
                        quantise(g_p[n1], pc[:, n1 * CHUNK : (n1 + 1) * CHUNK], ps[:, n1 * CHUNK : (n1 + 1) * CHUNK])
                if n2 < N_CH:
                    if jj == 2:
                        banks = word_transposes(raw_p[n2])
                    if jj == 3:
                        g_p[n2] = copy_out(banks)
            if c + 4 < N_CH:
                raw_p[c + 4] = load(rawp, pos_chunk(c + 4))
            elif c + 4 - N_CH < 4:
                raw_v[c + 4 - N_CH] = load(rawp, val_chunk(c + 4 - N_CH))
        root(4 * N_CH - 2)
        root(4 * N_CH - 1)
        acc = {}
        rb = {}
        gw = {}
        obank = {}

        def exps(i, h):
            nc.scalar.activation(out=dist[h][:, i, :], in_=dist[h][:, i, :], func=ACT.Exp, scale=-1.0)

        def partial_sums(i, h):
            if h == 0:
                acc[i] = psum.tile([P, 512], F32, tag="bank", name="acc")
            for t in range(16):
                nc.tensor.matmul(
                    out=acc[i][:, 0:P],
                    lhsT=dist[h][:, i, t * P : (t + 1) * P],
                    rhs=ident_f[:],
                    is_transpose=True,
                    start=(h == 0 and t == 0),
                    stop=(h == 1 and t == 15),
                )

        def row_sum(i):
            nc.scalar.activation(out=junk_r[:], in_=acc[i][:, 0:P], func=ACT.Identity, bias=1e-8 / P, accum_out=rsum[:, i : i + 1])

        def inverse(i):
            nc.vector.reciprocal(out=rinv[:, i : i + 1], in_=rsum[:, i : i + 1])
            rb[i] = psum.tile([P, 512], F32, tag="bank", name="rb")
            for c in range(4):
                nc.tensor.transpose(rb[i][:, c * P : (c + 1) * P], rinv[:, i : i + 1].to_broadcast([P, P]), ident_f[:])

        def multiply_on_gpsimd(i, h, lo, factor):
            n = 4 - lo
            nc.gpsimd.tensor_tensor(
                out=gw[(i, h)][:, lo * CHUNK :].rearrange("p (c m t) -> p c m t", c=n, t=4),
                in0=dist[h][:, i, :].rearrange("p (t c m) -> p c m t", t=4, c=4)[:, lo:4],
                in1=factor.unsqueeze(1).unsqueeze(3).to_broadcast([P, n, P, 4]),
                op=ALU.mult,
            )

        def multiply(i, h, lo, hi):
            factor = rb[i][:, 0 : (hi - lo) * P]
            nc.vector.tensor_tensor(
                out=gw[(i, h)][:, lo * CHUNK : hi * CHUNK].rearrange("p (b k t) -> p b t k", k=4, t=4),
                in0=dist[h][:, i, :].rearrange("p (t b k) -> p b t k", t=4, k=4)[:, lo * 32 : hi * 32],
                in1=factor.rearrange("p (b k) -> p b k", k=4).unsqueeze(2).to_broadcast([P, (hi - lo) * 32, 4, 4]),
                op=ALU.mult,
            )

        def weights(i):
            for h in range(2):
                gw[(i, h)] = grp.tile([P, 4 * CHUNK], BF16, tag="grouped", name="gw", align_bytes=64)
            rbs = rbp.tile([P, P], F32, tag="rbs", name="rbs")
            nc.vector.tensor_copy(out=rbs[:], in_=rb[i][:, 0:P])
            multiply_on_gpsimd(i, 1, 4 - SHARE, rbs[:])
            multiply(i, 0, 0, 4)
            if i < N_RT - 1:
                multiply(i, 1, 0, 4 - SHARE)
            else:
                multiply(i, 1, 0, 1)
                second(i, 0)
                multiply(i, 1, 1, 4 - SHARE)

        def second(i, h):
            wc = wcp.tile([P, CHUNK], U32, tag="wc", name="wc", align_bytes=64)
            ws = wcp.tile([P, CHUNK], U8, tag="ws", name="ws", align_bytes=64)
            quantise(gw[(i, h)], wc[:], ws[:])
            if h == 0:
                obank[i] = psum.tile([P, D], F32, tag="bank", name="obank")
            for cc in range(4):
                g = 4 * h + cc
                nc.tensor.matmul_mx(
                    out=obank[i][:],
                    lhsT=wc[:, cc * P : (cc + 1) * P].bitcast(FP8X4),
                    lhsT_scale=ws[:, cc * P : (cc + 1) * P],
                    rhs=vc[:, g * D : (g + 1) * D].bitcast(FP8X4),
                    rhs_scale=vs[:, g * D : (g + 1) * D],
                    start=(g == 0),
                    stop=(g == N_CH - 1),
                )

        def store(i):
            ost = outp.tile([P, D], F32, tag="ost", name="ost")
            if i < N_RT - 1:
                nc.scalar.copy(out=ost[:], in_=obank[i][:])
                nc.sync.dma_start(out=of[i // 4, i % 4], in_=ost[:])
            else:
                w = D // 2
                nc.scalar.copy(out=ost[:, 0:w], in_=obank[i][:, 0:w])
                nc.vector.tensor_copy(out=ost[:, w:D], in_=obank[i][:, w:D])
                nc.sync.dma_start(out=of[i // 4, i % 4, :, 0:w], in_=ost[:, 0:w])
                nc.sync.dma_start(out=of[i // 4, i % 4, :, w:D], in_=ost[:, w:D])

        def exp_tile(i):
            for h in range(2):
                exps(i, h)
                partial_sums(i, h)

        exp_tile(0)
        exps(1, 0)
        row_sum(0)
        for c in range(N_CH):
            values_a(c)
            if c > 0:
                values_b(c - 1)
        inverse(0)
        values_b(N_CH - 1)
        partial_sums(1, 0)
        exps(1, 1)
        partial_sums(1, 1)
        exps(2, 0)
        row_sum(1)
        exps(2, 1)
        for i in range(N_RT):
            weights(i)
            if i + 1 < N_RT:
                inverse(i + 1)
            if i + 2 < N_RT:
                partial_sums(i + 2, 0)
                partial_sums(i + 2, 1)
            if i + 3 < N_RT:
                exps(i + 3, 0)
            if i + 2 < N_RT:
                row_sum(i + 2)
            if i + 3 < N_RT:
                exps(i + 3, 1)
            if i < N_RT - 1:
                second(i, 0)
            second(i, 1)
            if i > 0:
                store(i - 1)
        store(N_RT - 1)
